import numpy as np
import ml_dtypes


def mxq(x, axis, fmt="e4m3"):
    dtype, down = {"e4m3": (ml_dtypes.float8_e4m3fn, 7), "e5m2": (ml_dtypes.float8_e5m2, 14)}[fmt]
    v = np.moveaxis(np.asarray(x, np.float32).astype(ml_dtypes.bfloat16).astype(np.float64), axis, -1)
    blocks = v.reshape(v.shape[:-1] + (-1, 32))
    amax = np.abs(blocks).max(-1, keepdims=True)
    byte = np.maximum(np.where(amax > 0, np.frexp(amax)[1] - 1 + 127, 0) - down, 1)
    scale = np.exp2(byte - 127.0)
    codes = (blocks / scale).astype(np.float32).astype(dtype).astype(np.float64)
    return np.moveaxis((codes * scale).reshape(v.shape), -1, axis)


WIDE = False


def mx_kscale(k):
    if not WIDE:
        return np.ones(k)
    levels = np.array([10, -10, 5, -5, 0])
    if k % 512:
        return np.exp2(np.random.permutation(np.resize(levels, k // 32))).repeat(32)
    a = np.empty((k // 512, 16))
    for p in range(k // 512):
        a[p, :8] = np.random.permutation(np.resize(levels, 8))
        for g in range(8):
            far = levels[np.abs(levels - a[p, g]) >= 10]
            a[p, g + 8] = far[np.random.randint(len(far))]
    return np.exp2(a.ravel()).repeat(32)


BF16 = ml_dtypes.bfloat16


def bf(x):
    return np.asarray(x, np.float32).astype(BF16)


def f64(x):
    return np.asarray(x).astype(np.float64)


BS, H, XDIM = 8192, 128, 256
IN = XDIM + 2 * H


def sigmoid(v):
    return 1.0 / (1.0 + np.exp(-v))


def setup_inputs():
    s = mx_kscale(IN)
    c = 1.0 / np.sqrt(IN)

    def draw_w():
        return bf(np.random.standard_normal((H, IN)) * c / s[None, :])

    def draw_b():
        return bf(np.random.standard_normal(H) * 0.3)

    return {
        "input_x": bf(np.random.standard_normal((BS, XDIM)) * s[:XDIM]),
        "previous_time": bf(np.random.standard_normal((BS, H)) * s[XDIM:XDIM + H]),
        "previous_layer": bf(np.random.standard_normal((BS, H)) * s[XDIM + H:]),
        "old_state": bf(np.random.standard_normal((BS, H)) * 0.5),
        "Wi": draw_w(), "bi": draw_b(),
        "Wf": draw_w(), "bf": draw_b(),
        "Wo": draw_w(), "bo": draw_b(),
        "Ws": draw_w(), "bs_state": draw_b(),
    }


def reference(input_x, previous_time, previous_layer, old_state, Wi, bi, Wf, bf, Wo, bo, Ws, bs_state):
    z = np.concatenate([f64(input_x), f64(previous_time), f64(previous_layer)], axis=1)
    W_all = np.concatenate([f64(Wi), f64(Wf), f64(Wo), f64(Ws)], axis=0)
    b_all = np.concatenate([f64(bi), f64(bf), f64(bo), f64(bs_state)], axis=0)
    proj = (mxq(z, 1, "e4m3") @ mxq(W_all, 1, "e4m3").T) + b_all
    gi, gf, go, gs = np.split(proj, 4, axis=1)
    input_gate = sigmoid(gi)
    forget_gate = sigmoid(gf)
    output_gate = sigmoid(go)
    new_state = forget_gate * f64(old_state) + input_gate * np.tanh(gs)
    new_hidden = output_gate * np.tanh(new_state)
    return new_hidden

@@ -1,0 +1,301 @@
+from contextlib import ExitStack
+
+import concourse.bass as bass
+import concourse.mybir as mybir
+import concourse.tile as tile
+from concourse.masks import make_identity
+
+F32 = mybir.dt.float32
+BF16 = mybir.dt.bfloat16
+U32 = mybir.dt.uint32
+U8 = mybir.dt.uint8
+FP8X4 = mybir.dt.float8_e4m3fn_x4
+ACT = mybir.ActivationFunctionType
+ALU = mybir.AluOpType
+
+P = 128
+BS, H, XDIM = 8192, 128, 256
+IN = XDIM + 2 * H
+NT = BS // P
+FLOPS = 2 * BS * IN * 4 * H
+
+CHUNKS = [4] * 16
+LOADS = [4, 4, 4, 4, 8, 8, 8, 8, 8, 8]
+OLD_LAG = 1
+CMODE = ["G", "ACC"]
+
+
+def tile_rnn_unit_t_kernel(tc, input_x, previous_time, previous_layer, old_state,
+                                      Wi, bi, Wf, bf, Wo, bo, Ws, bs_state, out):
+    nc = tc.nc
+    n_chunks = len(CHUNKS)
+    starts = [sum(CHUNKS[:n]) for n in range(n_chunks)]
+    assert sum(CHUNKS) == NT and sum(LOADS) == NT
+
+    x_v = input_x.rearrange("(p t) k -> p t k", t=NT)
+    pt_v = previous_time.rearrange("(p t) k -> p t k", t=NT)
+    pl_v = previous_layer.rearrange("(p t) k -> p t k", t=NT)
+    old_v = old_state.rearrange("(p t) k -> p (t k)", t=NT)
+    out_v = out.rearrange("(p t) h -> p (t h)", t=NT)
+
+    with ExitStack() as ctx:
+        const = ctx.enter_context(tc.tile_pool(name="const", bufs=1))
+        res = ctx.enter_context(tc.tile_pool(name="res", bufs=1))
+        ring = ctx.enter_context(tc.tile_pool(name="ring", bufs=4))
+        psum = ctx.enter_context(tc.psum_pool(name="psum", bufs=8))
+        ctx.enter_context(tc.manual_schedule())
+
+        brow = const.tile([P, P], BF16, name="brow")
+        nc.vector.memset(brow[:], 0.0)
+        warm = const.tile([P, 1], F32, name="warm")
+        nc.vector.memset(warm[:], 0.0)
+        nc.scalar.activation(out=warm[:], in_=warm[:], func=ACT.Sigmoid)
+        ident_f = const.tile([P, P], F32, name="ident_f")
+        make_identity(nc, ident_f[:])
+
+        group_of = {}
+        zg, og = [], []
+        bounds = [(sum(LOADS[:g]), sum(LOADS[:g + 1])) for g in range(len(LOADS))]
+
+        def load_group(g):
+            a, b = bounds[g]
+            n = b - a
+            zt = res.tile([P, n * IN], BF16, name="z%d" % g)
+            zt3 = zt[:].rearrange("p (t k) -> p t k", k=IN)
+            nc.sync.dma_start(out=zt3[:, :, 0:XDIM], in_=x_v[:, a:b, :])
+            nc.sync.dma_start(out=zt3[:, :, XDIM:XDIM + H], in_=pt_v[:, a:b, :])
+            nc.sync.dma_start(out=zt3[:, :, XDIM + H:IN], in_=pl_v[:, a:b, :])
+            zg.append(zt)
+            for t in range(a, b):
+                group_of[t] = (g, t - a)
+
+        def load_old(g):
+            a, b = bounds[g]
+            ot = res.tile([P, (b - a) * H], BF16, name="old%d" % g)
+            nc.sync.dma_start(out=ot[:], in_=old_v[:, a * H:b * H])
+            og.append(ot)
+
+        def bias_row(eng, g):
+            eng.dma_start(out=brow[g:g + 1, :], in_=b_dram[g].rearrange("(o h) -> o h", o=1))
+
+        w_dram = [Wi, Ws, Wf, Wo]
+        b_dram = [bi, bs_state, bf, bo]
+        load_group(0)
+        w_sb = []
+        for g in range(4):
+            wt = const.tile([P, IN], BF16, name="w%d" % g)
+            nc.sync.dma_start(out=wt[:], in_=w_dram[g])
+            w_sb.append(wt)
+        for g in range(4):
+            bias_row(nc.sync, g)
+        ident_b = const.tile([P, P], BF16, name="ident_b")
+        make_identity(nc, ident_b[:])
+        for g in range(1, len(LOADS) + OLD_LAG):
+            if g < len(LOADS):
+                load_group(g)
+            if g >= OLD_LAG:
+                load_old(g - OLD_LAG)
+
+        w_q = {}
+
+        def wt_stage(h):
+            wz = psum.tile([P, 2, 2 * P], F32, name="wz", tag="bank")
+            for gg in range(2):
+                words = w_sb[2 * h + gg][:].bitcast(F32)
+                for u in range(2):
+                    nc.tensor.transpose(out=wz[:, u, gg * P:(gg + 1) * P], in_=words[:, u:2 * P:2],
+                                        identity=ident_f[:])
+            wgrp = const.tile([P, 8 * P], BF16, name="wgrp%d" % h, align_bytes=64)
+            nc.scalar.copy(out=wgrp[:].bitcast(F32).rearrange("p (c u) -> p c u", u=2),
+                           in_=wz[:].rearrange("p u c -> p c u"))
+            w_q[h] = wgrp
+
+        def wq_stage(h):
+            wc = const.tile([P, 2 * P], U32, name="wc%d" % h, align_bytes=64)
+            ws = const.tile([P, 2 * P], U8, name="ws%d" % h, align_bytes=64)
+            nc.vector.quantize_mx(out=wc[:].bitcast(FP8X4), scales=ws[:], in_=w_q[h][:])
+            w_q[h] = (wc, ws)
+
+        bias = const.tile([P, 4], F32, name="bias")
+
+        st = {}
+
+        def ok(n):
+            return 0 <= n < n_chunks
+
+        def zt_stage(n):
+            if not ok(n):
+                return
+            w = CHUNKS[n]
+            banks = []
+            for h in range((w + 1) // 2):
+                wb = min(2, w - 2 * h)
+                zb = psum.tile([P, 2, wb * P], F32, name="zb", tag="bank")
+                for j in range(wb):
+                    g, r = group_of[starts[n] + 2 * h + j]
+                    words = zg[g][:].bitcast(F32)
+                    for u in range(2):
+                        nc.tensor.transpose(out=zb[:, u, j * P:(j + 1) * P],
+                                            in_=words[:, 2 * r * P + u:2 * (r + 1) * P:2],
+                                            identity=ident_f[:])
+                banks.append((zb, wb))
+            st["zb", n] = banks
+            grp = ring.tile([P, w * 4 * P], BF16, name="grp", tag="grp", align_bytes=64)
+            st["grp", n] = grp
+
+        def zc_stage(n):
+            if not ok(n):
+                return
+            gw = st["grp", n][:].bitcast(F32)
+            c0 = 0
+            for zb, wb in st["zb", n]:
+                nc.vector.tensor_copy(out=gw[:, 2 * c0:2 * (c0 + wb * P)].rearrange("p (c u) -> p c u", u=2),
+                                      in_=zb[:].rearrange("p u c -> p c u"))
+                c0 += wb * P
+
+        def q_stage(n):
+            if not ok(n):
+                return
+            w = CHUNKS[n]
+            codes = ring.tile([P, w * P], U32, name="codes", tag="codes", align_bytes=64)
+            scl = ring.tile([P, w * P], U8, name="scl", tag="scl", align_bytes=64)
+            nc.vector.quantize_mx(out=codes[:].bitcast(FP8X4), scales=scl[:], in_=st["grp", n][:])
+            st["codes", n] = (codes, scl)
+
+        def mx_stage(n):
+            if not ok(n):
+                return
+            w = CHUNKS[n]
+            codes, scl = st["codes", n]
+            for g in range(4):
+                gb = psum.tile([P, w * P], F32, name="gb", tag="bank")
+                wc, ws = w_q[g // 2]
+                cols = slice((g % 2) * P, (g % 2 + 1) * P)
+                nc.tensor.matmul_mx(out=gb[:], lhsT=wc[:, cols].bitcast(FP8X4), lhsT_scale=ws[:, cols],
+                                    rhs=codes[:].bitcast(FP8X4), rhs_scale=scl[:], start=True, stop=True)
+                st["gb", n, g] = gb
+
+        def act_stage(n):
+            if not ok(n):
+                return
+            w = CHUNKS[n]
+            for g in range(4):
+                a = ring.tile([P, w * P], F32, name="gate%d" % g, tag="gate%d" % g)
+                nc.scalar.activation(out=a[:], in_=st["gb", n, g][:], func=(ACT.Tanh if g == 1 else ACT.Sigmoid),
+                                     bias=bias[:, g:g + 1], scale=1.0)
+                st["gate", n, g] = a
+
+        def ot_stage(n):
+            if not ok(n):
+                return
+            w = CHUNKS[n]
+            ob = psum.tile([P, w * P], BF16, name="ob", tag="bank")
+            for j in range(w):
+                g, r = group_of[starts[n] + j]
+                nc.tensor.transpose(out=ob[:, j * P:(j + 1) * P], in_=og[g][:, r * P:(r + 1) * P],
+                                    identity=ident_b[:])
+            st["ob", n] = ob
+
+        def a_stage(n):
+            if not ok(n):
+                return
+            w = CHUNKS[n]
+            a = ring.tile([P, w * P], F32, name="fa", tag="fa")
+            nc.vector.tensor_tensor(out=a[:], in0=st["gate", n, 2][:], in1=st["ob", n][:], op=ALU.mult)
+            st["A", n] = a
+
+        def b_stage(n):
+            if not ok(n):
+                return
+            w = CHUNKS[n]
+            b = ring.tile([P, w * P], F32, name="ig", tag="ig")
+            nc.gpsimd.tensor_tensor(out=b[:], in0=st["gate", n, 0][:], in1=st["gate", n, 1][:], op=ALU.mult)
+            st["B", n] = b
+
+        def cmode(n):
+            return CMODE[n % len(CMODE)]
+
+        def c_stage(n):
+            if not ok(n) or cmode(n) == "ACC":
+                return
+            w = CHUNKS[n]
+            c = ring.tile([P, w * P], F32, name="cs", tag="cs")
+            eng = nc.vector if cmode(n) == "V" else nc.gpsimd
+            eng.tensor_tensor(out=c[:], in0=st["A", n][:], in1=st["B", n][:], op=ALU.add)
+            st["C", n] = c
+
+        def ct_stage(n):
+            if not ok(n):
+                return
+            w = CHUNKS[n]
+            cb = psum.tile([P, w * P], F32, name="cb", tag="bank")
+            for j in range(w):
+                cols = slice(j * P, (j + 1) * P)
+                if cmode(n) == "ACC":
+                    nc.tensor.matmul(out=cb[:, cols], lhsT=st["A", n][:, cols], rhs=ident_f[:],
+                                     is_transpose=True, start=True, stop=False)
+                    nc.tensor.matmul(out=cb[:, cols], lhsT=st["B", n][:, cols], rhs=ident_f[:],
+                                     is_transpose=True, start=False, stop=True)
+                else:
+                    nc.tensor.transpose(out=cb[:, cols], in_=st["C", n][:, cols], identity=ident_f[:])
+            st["cb", n] = cb
+
+        def oot_stage(n):
+            if not ok(n):
+                return
+            w = CHUNKS[n]
+            oo = psum.tile([P, w * P], F32, name="oo", tag="bank")
+            for j in range(w):
+                cols = slice(j * P, (j + 1) * P)
+                nc.tensor.transpose(out=oo[:, cols], in_=st["gate", n, 3][:, cols], identity=ident_f[:])
+            st["oo", n] = oo
+
+        def th_stage(n):
+            if not ok(n):
+                return
+            w = CHUNKS[n]
+            th = ring.tile([P, w * P], F32, name="th", tag="th")
+            nc.scalar.activation(out=th[:], in_=st["cb", n][:], func=ACT.Tanh)
+            st["th", n] = th
+
+        def out_stage(n):
+            if not ok(n):
+                return
+            w = CHUNKS[n]
+            cols = slice(starts[n] * H, (starts[n] + w) * H)
+            res_t = res.tile([P, w * H], F32, name="out%d" % n)
+            nc.vector.tensor_tensor(out=res_t[:], in0=st["th", n][:], in1=st["oo", n][:], op=ALU.mult)
+            nc.sync.dma_start(out=out_v[:, cols], in_=res_t[:])
+
+        zt_stage(0)
+        wt_stage(0)
+        zc_stage(0)
+        wt_stage(1)
+        wq_stage(0)
+        q_stage(0)
+        wq_stage(1)
+        zt_stage(1)
+        bias_ps = psum.tile([P, P], BF16, name="bias_ps", tag="bank")
+        nc.tensor.transpose(out=bias_ps[:], in_=brow[:], identity=ident_b[:])
+        nc.scalar.copy(out=bias[:], in_=bias_ps[:, 0:4])
+        zc_stage(1)
+        q_stage(1)
+        for k in range(n_chunks + 2):
+            mx_stage(k)
+            act_stage(k)
+            out_stage(k - 2)
+            zt_stage(k + 2)
+            ot_stage(k)
+            if cmode(k - 1) == "ACC":
+                ct_stage(k - 1)
+                oot_stage(k - 1)
+            else:
+                oot_stage(k - 1)
+            b_stage(k)
+            zc_stage(k + 2)
+            a_stage(k)
+            c_stage(k)
+            if cmode(k - 1) != "ACC":
+                ct_stage(k - 1)
+            th_stage(k - 1)
+            q_stage(k + 2)

@@ -20,7 +20,7 @@ NT = BS // P
 FLOPS = 2 * BS * IN * 4 * H
 
 CHUNKS = [4] * 16
-LOADS = [4, 4, 4, 4, 8, 8, 8, 8, 8, 8]
+LOADS = [4] * 16
 OLD_LAG = 1
 CMODE = ["G", "ACC"]
 
@@ -32,11 +32,11 @@ def tile_rnn_unit_t_kernel(tc, input_x, previous_time, previous_layer, old_state
     starts = [sum(CHUNKS[:n]) for n in range(n_chunks)]
     assert sum(CHUNKS) == NT and sum(LOADS) == NT
 
-    x_v = input_x.rearrange("(p t) k -> p t k", t=NT)
-    pt_v = previous_time.rearrange("(p t) k -> p t k", t=NT)
-    pl_v = previous_layer.rearrange("(p t) k -> p t k", t=NT)
-    old_v = old_state.rearrange("(p t) k -> p (t k)", t=NT)
-    out_v = out.rearrange("(p t) h -> p (t h)", t=NT)
+    x_v = input_x.rearrange("(c p t) k -> c p t k", p=P, t=4)
+    pt_v = previous_time.rearrange("(c p t) k -> c p t k", p=P, t=4)
+    pl_v = previous_layer.rearrange("(c p t) k -> c p t k", p=P, t=4)
+    old_v = old_state.rearrange("(c p t) k -> c p (t k)", p=P, t=4)
+    out_v = out.rearrange("(c p t) h -> c p (t h)", p=P, t=4)
 
     with ExitStack() as ctx:
         const = ctx.enter_context(tc.tile_pool(name="const", bufs=1))
@@ -62,9 +62,9 @@ def tile_rnn_unit_t_kernel(tc, input_x, previous_time, previous_layer, old_state
             n = b - a
             zt = res.tile([P, n * IN], BF16, name="z%d" % g)
             zt3 = zt[:].rearrange("p (t k) -> p t k", k=IN)
-            nc.sync.dma_start(out=zt3[:, :, 0:XDIM], in_=x_v[:, a:b, :])
-            nc.sync.dma_start(out=zt3[:, :, XDIM:XDIM + H], in_=pt_v[:, a:b, :])
-            nc.sync.dma_start(out=zt3[:, :, XDIM + H:IN], in_=pl_v[:, a:b, :])
+            nc.sync.dma_start(out=zt3[:, :, 0:XDIM], in_=x_v[g])
+            nc.sync.dma_start(out=zt3[:, :, XDIM:XDIM + H], in_=pt_v[g])
+            nc.sync.dma_start(out=zt3[:, :, XDIM + H:IN], in_=pl_v[g])
             zg.append(zt)
             for t in range(a, b):
                 group_of[t] = (g, t - a)
@@ -72,7 +72,7 @@ def tile_rnn_unit_t_kernel(tc, input_x, previous_time, previous_layer, old_state
         def load_old(g):
             a, b = bounds[g]
             ot = res.tile([P, (b - a) * H], BF16, name="old%d" % g)
-            nc.sync.dma_start(out=ot[:], in_=old_v[:, a * H:b * H])
+            nc.sync.dma_start(out=ot[:], in_=old_v[g])
             og.append(ot)
 
         def bias_row(eng, g):
@@ -262,10 +262,9 @@ def tile_rnn_unit_t_kernel(tc, input_x, previous_time, previous_layer, old_state
             if not ok(n):
                 return
             w = CHUNKS[n]
-            cols = slice(starts[n] * H, (starts[n] + w) * H)
             res_t = res.tile([P, w * H], F32, name="out%d" % n)
             nc.vector.tensor_tensor(out=res_t[:], in0=st["th", n][:], in1=st["oo", n][:], op=ALU.mult)
-            nc.sync.dma_start(out=out_v[:, cols], in_=res_t[:])
+            nc.sync.dma_start(out=out_v[n], in_=res_t[:])
 
         zt_stage(0)
         wt_stage(0)

@@ -22,7 +22,7 @@ FLOPS = 2 * BS * IN * 4 * H
 CHUNKS = [4] * 16
 LOADS = [4] * 16
 OLD_LAG = 1
-CMODE = ["G", "ACC"]
+CMODE = ["V", "ACC"]
 
 
 def tile_rnn_unit_t_kernel(tc, input_x, previous_time, previous_layer, old_state,
@@ -189,11 +189,11 @@ def tile_rnn_unit_t_kernel(tc, input_x, previous_time, previous_layer, old_state
             if not ok(n):
                 return
             w = CHUNKS[n]
-            ob = psum.tile([P, w * P], BF16, name="ob", tag="bank")
+            ob = psum.tile([P, w * P], F32, name="ob", tag="bank")
             for j in range(w):
                 g, r = group_of[starts[n] + j]
-                nc.tensor.transpose(out=ob[:, j * P:(j + 1) * P], in_=og[g][:, r * P:(r + 1) * P],
-                                    identity=ident_b[:])
+                nc.tensor.matmul(out=ob[:, j * P:(j + 1) * P], lhsT=og[g][:, r * P:(r + 1) * P],
+                                 rhs=ident_b[:], start=True, stop=True)
             st["ob", n] = ob
 
         def a_stage(n):
@@ -282,19 +282,14 @@ def tile_rnn_unit_t_kernel(tc, input_x, previous_time, previous_layer, old_state
         for k in range(n_chunks + 2):
             mx_stage(k)
             act_stage(k)
-            out_stage(k - 2)
             zt_stage(k + 2)
             ot_stage(k)
-            if cmode(k - 1) == "ACC":
-                ct_stage(k - 1)
-                oot_stage(k - 1)
-            else:
-                oot_stage(k - 1)
+            oot_stage(k - 2)
+            ct_stage(k - 1)
+            th_stage(k - 1)
             b_stage(k)
             zc_stage(k + 2)
+            out_stage(k - 2)
             a_stage(k)
-            c_stage(k)
-            if cmode(k - 1) != "ACC":
-                ct_stage(k - 1)
-            th_stage(k - 1)
             q_stage(k + 2)
+            c_stage(k)

from contextlib import ExitStack

import concourse.bass as bass
import concourse.mybir as mybir
import concourse.tile as tile
from concourse.masks import make_identity

F32 = mybir.dt.float32
BF16 = mybir.dt.bfloat16
U32 = mybir.dt.uint32
U8 = mybir.dt.uint8
FP8X4 = mybir.dt.float8_e4m3fn_x4
ACT = mybir.ActivationFunctionType
ALU = mybir.AluOpType

P = 128
BS, H, XDIM = 8192, 128, 256
IN = XDIM + 2 * H
NT = BS // P
FLOPS = 2 * BS * IN * 4 * H

CHUNKS = [4] * 16
LOADS = [4] * 16
OLD_LAG = 1
CMODE = ["V", "ACC"]


def tile_rnn_unit_t_kernel(tc, input_x, previous_time, previous_layer, old_state,
                                      Wi, bi, Wf, bf, Wo, bo, Ws, bs_state, out):
    nc = tc.nc
    n_chunks = len(CHUNKS)
    starts = [sum(CHUNKS[:n]) for n in range(n_chunks)]
    assert sum(CHUNKS) == NT and sum(LOADS) == NT

    x_v = input_x.rearrange("(c p t) k -> c p t k", p=P, t=4)
    pt_v = previous_time.rearrange("(c p t) k -> c p t k", p=P, t=4)
    pl_v = previous_layer.rearrange("(c p t) k -> c p t k", p=P, t=4)
    old_v = old_state.rearrange("(c p t) k -> c p (t k)", p=P, t=4)
    out_v = out.rearrange("(c p t) h -> c p (t h)", p=P, t=4)

    with ExitStack() as ctx:
        const = ctx.enter_context(tc.tile_pool(name="const", bufs=1))
        res = ctx.enter_context(tc.tile_pool(name="res", bufs=1))
        ring = ctx.enter_context(tc.tile_pool(name="ring", bufs=4))
        psum = ctx.enter_context(tc.psum_pool(name="psum", bufs=8))
        ctx.enter_context(tc.manual_schedule())

        brow = const.tile([P, P], BF16, name="brow")
        nc.vector.memset(brow[:], 0.0)
        warm = const.tile([P, 1], F32, name="warm")
        nc.vector.memset(warm[:], 0.0)
        nc.scalar.activation(out=warm[:], in_=warm[:], func=ACT.Sigmoid)
        ident_f = const.tile([P, P], F32, name="ident_f")
        make_identity(nc, ident_f[:])

        group_of = {}
        zg, og = [], []
        bounds = [(sum(LOADS[:g]), sum(LOADS[:g + 1])) for g in range(len(LOADS))]

        def load_group(g):
            a, b = bounds[g]
            n = b - a
            zt = res.tile([P, n * IN], BF16, name="z%d" % g)
            zt3 = zt[:].rearrange("p (t k) -> p t k", k=IN)
            nc.sync.dma_start(out=zt3[:, :, 0:XDIM], in_=x_v[g])
            nc.sync.dma_start(out=zt3[:, :, XDIM:XDIM + H], in_=pt_v[g])
            nc.sync.dma_start(out=zt3[:, :, XDIM + H:IN], in_=pl_v[g])
            zg.append(zt)
            for t in range(a, b):
                group_of[t] = (g, t - a)

        def load_old(g):
            a, b = bounds[g]
            ot = res.tile([P, (b - a) * H], BF16, name="old%d" % g)
            nc.sync.dma_start(out=ot[:], in_=old_v[g])
            og.append(ot)

        def bias_row(eng, g):
            eng.dma_start(out=brow[g:g + 1, :], in_=b_dram[g].rearrange("(o h) -> o h", o=1))

        w_dram = [Wi, Ws, Wf, Wo]
        b_dram = [bi, bs_state, bf, bo]
        load_group(0)
        w_sb = []
        for g in range(4):
            wt = const.tile([P, IN], BF16, name="w%d" % g)
            nc.sync.dma_start(out=wt[:], in_=w_dram[g])
            w_sb.append(wt)
        for g in range(4):
            bias_row(nc.sync, g)
        ident_b = const.tile([P, P], BF16, name="ident_b")
        make_identity(nc, ident_b[:])
        for g in range(1, len(LOADS) + OLD_LAG):
            if g < len(LOADS):
                load_group(g)
            if g >= OLD_LAG:
                load_old(g - OLD_LAG)

        w_q = {}

        def wt_stage(h):
            wz = psum.tile([P, 2, 2 * P], F32, name="wz", tag="bank")
            for gg in range(2):
                words = w_sb[2 * h + gg][:].bitcast(F32)
                for u in range(2):
                    nc.tensor.transpose(out=wz[:, u, gg * P:(gg + 1) * P], in_=words[:, u:2 * P:2],
                                        identity=ident_f[:])
            wgrp = const.tile([P, 8 * P], BF16, name="wgrp%d" % h, align_bytes=64)
            nc.scalar.copy(out=wgrp[:].bitcast(F32).rearrange("p (c u) -> p c u", u=2),
                           in_=wz[:].rearrange("p u c -> p c u"))
            w_q[h] = wgrp

        def wq_stage(h):
            wc = const.tile([P, 2 * P], U32, name="wc%d" % h, align_bytes=64)
            ws = const.tile([P, 2 * P], U8, name="ws%d" % h, align_bytes=64)
            nc.vector.quantize_mx(out=wc[:].bitcast(FP8X4), scales=ws[:], in_=w_q[h][:])
            w_q[h] = (wc, ws)

        bias = const.tile([P, 4], F32, name="bias")

        st = {}

        def ok(n):
            return 0 <= n < n_chunks

        def zt_stage(n):
            if not ok(n):
                return
            w = CHUNKS[n]
            banks = []
            for h in range((w + 1) // 2):
                wb = min(2, w - 2 * h)
                zb = psum.tile([P, 2, wb * P], F32, name="zb", tag="bank")
                for j in range(wb):
                    g, r = group_of[starts[n] + 2 * h + j]
                    words = zg[g][:].bitcast(F32)
                    for u in range(2):
                        nc.tensor.transpose(out=zb[:, u, j * P:(j + 1) * P],
                                            in_=words[:, 2 * r * P + u:2 * (r + 1) * P:2],
                                            identity=ident_f[:])
                banks.append((zb, wb))
            st["zb", n] = banks
            grp = ring.tile([P, w * 4 * P], BF16, name="grp", tag="grp", align_bytes=64)
            st["grp", n] = grp

        def zc_stage(n):
            if not ok(n):
                return
            gw = st["grp", n][:].bitcast(F32)
            c0 = 0
            for zb, wb in st["zb", n]:
                nc.vector.tensor_copy(out=gw[:, 2 * c0:2 * (c0 + wb * P)].rearrange("p (c u) -> p c u", u=2),
                                      in_=zb[:].rearrange("p u c -> p c u"))
                c0 += wb * P

        def q_stage(n):
            if not ok(n):
                return
            w = CHUNKS[n]
            codes = ring.tile([P, w * P], U32, name="codes", tag="codes", align_bytes=64)
            scl = ring.tile([P, w * P], U8, name="scl", tag="scl", align_bytes=64)
            nc.vector.quantize_mx(out=codes[:].bitcast(FP8X4), scales=scl[:], in_=st["grp", n][:])
            st["codes", n] = (codes, scl)

        def mx_stage(n):
            if not ok(n):
                return
            w = CHUNKS[n]
            codes, scl = st["codes", n]
            for g in range(4):
                gb = psum.tile([P, w * P], F32, name="gb", tag="bank")
                wc, ws = w_q[g // 2]
                cols = slice((g % 2) * P, (g % 2 + 1) * P)
                nc.tensor.matmul_mx(out=gb[:], lhsT=wc[:, cols].bitcast(FP8X4), lhsT_scale=ws[:, cols],
                                    rhs=codes[:].bitcast(FP8X4), rhs_scale=scl[:], start=True, stop=True)
                st["gb", n, g] = gb

        def act_stage(n):
            if not ok(n):
                return
            w = CHUNKS[n]
            for g in range(4):
                a = ring.tile([P, w * P], F32, name="gate%d" % g, tag="gate%d" % g)
                nc.scalar.activation(out=a[:], in_=st["gb", n, g][:], func=(ACT.Tanh if g == 1 else ACT.Sigmoid),
                                     bias=bias[:, g:g + 1], scale=1.0)
                st["gate", n, g] = a

        def ot_stage(n):
            if not ok(n):
                return
            w = CHUNKS[n]
            ob = psum.tile([P, w * P], F32, name="ob", tag="bank")
            for j in range(w):
                g, r = group_of[starts[n] + j]
                nc.tensor.matmul(out=ob[:, j * P:(j + 1) * P], lhsT=og[g][:, r * P:(r + 1) * P],
                                 rhs=ident_b[:], start=True, stop=True)
            st["ob", n] = ob

        def a_stage(n):
            if not ok(n):
                return
            w = CHUNKS[n]
            a = ring.tile([P, w * P], F32, name="fa", tag="fa")
            nc.vector.tensor_tensor(out=a[:], in0=st["gate", n, 2][:], in1=st["ob", n][:], op=ALU.mult)
            st["A", n] = a

        def b_stage(n):
            if not ok(n):
                return
            w = CHUNKS[n]
            b = ring.tile([P, w * P], F32, name="ig", tag="ig")
            nc.gpsimd.tensor_tensor(out=b[:], in0=st["gate", n, 0][:], in1=st["gate", n, 1][:], op=ALU.mult)
            st["B", n] = b

        def cmode(n):
            return CMODE[n % len(CMODE)]

        def c_stage(n):
            if not ok(n) or cmode(n) == "ACC":
                return
            w = CHUNKS[n]
            c = ring.tile([P, w * P], F32, name="cs", tag="cs")
            eng = nc.vector if cmode(n) == "V" else nc.gpsimd
            eng.tensor_tensor(out=c[:], in0=st["A", n][:], in1=st["B", n][:], op=ALU.add)
            st["C", n] = c

        def ct_stage(n):
            if not ok(n):
                return
            w = CHUNKS[n]
            cb = psum.tile([P, w * P], F32, name="cb", tag="bank")
            for j in range(w):
                cols = slice(j * P, (j + 1) * P)
                if cmode(n) == "ACC":
                    nc.tensor.matmul(out=cb[:, cols], lhsT=st["A", n][:, cols], rhs=ident_f[:],
                                     is_transpose=True, start=True, stop=False)
                    nc.tensor.matmul(out=cb[:, cols], lhsT=st["B", n][:, cols], rhs=ident_f[:],
                                     is_transpose=True, start=False, stop=True)
                else:
                    nc.tensor.transpose(out=cb[:, cols], in_=st["C", n][:, cols], identity=ident_f[:])
            st["cb", n] = cb

        def oot_stage(n):
            if not ok(n):
                return
            w = CHUNKS[n]
            oo = psum.tile([P, w * P], F32, name="oo", tag="bank")
            for j in range(w):
                cols = slice(j * P, (j + 1) * P)
                nc.tensor.transpose(out=oo[:, cols], in_=st["gate", n, 3][:, cols], identity=ident_f[:])
            st["oo", n] = oo

        def th_stage(n):
            if not ok(n):
                return
            w = CHUNKS[n]
            th = ring.tile([P, w * P], F32, name="th", tag="th")
            nc.scalar.activation(out=th[:], in_=st["cb", n][:], func=ACT.Tanh)
            st["th", n] = th

        def out_stage(n):
            if not ok(n):
                return
            w = CHUNKS[n]
            res_t = res.tile([P, w * H], F32, name="out%d" % n)
            nc.vector.tensor_tensor(out=res_t[:], in0=st["th", n][:], in1=st["oo", n][:], op=ALU.mult)
            nc.sync.dma_start(out=out_v[n], in_=res_t[:])

        zt_stage(0)
        wt_stage(0)
        zc_stage(0)
        wt_stage(1)
        wq_stage(0)
        q_stage(0)
        wq_stage(1)
        zt_stage(1)
        bias_ps = psum.tile([P, P], BF16, name="bias_ps", tag="bank")
        nc.tensor.transpose(out=bias_ps[:], in_=brow[:], identity=ident_b[:])
        nc.scalar.copy(out=bias[:], in_=bias_ps[:, 0:4])
        zc_stage(1)
        q_stage(1)
        for k in range(n_chunks + 2):
            mx_stage(k)
            act_stage(k)
            zt_stage(k + 2)
            ot_stage(k)
            oot_stage(k - 2)
            ct_stage(k - 1)
            th_stage(k - 1)
            b_stage(k)
            zc_stage(k + 2)
            out_stage(k - 2)
            a_stage(k)
            q_stage(k + 2)
            c_stage(k)
